import numpy as np
import ml_dtypes


def mxq(x, axis, fmt="e4m3"):
    dtype, down = {"e4m3": (ml_dtypes.float8_e4m3fn, 7), "e5m2": (ml_dtypes.float8_e5m2, 14)}[fmt]
    v = np.moveaxis(np.asarray(x, np.float32).astype(ml_dtypes.bfloat16).astype(np.float64), axis, -1)
    blocks = v.reshape(v.shape[:-1] + (-1, 32))
    amax = np.abs(blocks).max(-1, keepdims=True)
    byte = np.maximum(np.where(amax > 0, np.frexp(amax)[1] - 1 + 127, 0) - down, 1)
    scale = np.exp2(byte - 127.0)
    codes = (blocks / scale).astype(np.float32).astype(dtype).astype(np.float64)
    return np.moveaxis((codes * scale).reshape(v.shape), -1, axis)


WIDE = False


def mx_kscale(k):
    if not WIDE:
        return np.ones(k)
    levels = np.array([10, -10, 5, -5, 0])
    a = np.random.permutation(np.resize(levels, k // 512 * 4)).reshape(k // 512, 4)
    idx = np.arange(k)
    return np.exp2(a[idx // 512, idx % 128 // 32])


BF16 = ml_dtypes.bfloat16


def bf(x):
    return np.asarray(x, np.float32).astype(BF16)


def f64(x):
    return np.asarray(x).astype(np.float64)


B, C, H, WI, D, N = 4096, 1, 32, 32, 512, 512
F = C * H * WI
MARGIN, SCALE = 50.0, 5.0
TARGET = 51.5
LN = np.log(N)
ZN = np.sqrt(2.0 * LN) - (np.log(LN) + np.log(4.0 * np.pi)) / (2.0 * np.sqrt(2.0 * LN))
SIG = TARGET / np.sqrt(2.0 * D - ZN * np.sqrt(6.0 * D))


def setup_inputs():
    s = mx_kscale(F)
    x = bf((np.random.standard_normal((B, F)) * s).reshape(B, C, H, WI))
    y = bf(f64(x) + 1.4 * np.random.standard_normal((B, C, H, WI)))
    W = bf(np.random.standard_normal((F, D)) * SIG / np.sqrt(F) / s[:, None])
    lookup = bf(np.random.standard_normal((N, D)) * SIG)
    return {"x": x, "y": y, "W": W, "lookup": lookup}


def reference(x, y, W, lookup):
    x, y, W, lookup = f64(x), f64(y), f64(W), f64(lookup)
    nb = x.shape[0]
    emb = mxq(x.reshape(nb, -1), 1, "e4m3") @ mxq(W, 0, "e4m3")
    sq = (
        np.sum(emb * emb, axis=-1)[:, None]
        + np.sum(lookup * lookup, axis=-1)[None, :]
        - 2.0 * (mxq(emb, 1, "e4m3") @ mxq(lookup, 1, "e4m3").T)
    )
    dist = np.sqrt(np.maximum(sq, 0.0))
    min_d = np.min(dist, axis=1)
    mse = np.mean((x - y) ** 2)
    return mse + np.minimum(MARGIN - min_d, 0.0) * SCALE

@@ -1,0 +1,288 @@
+from contextlib import ExitStack
+
+import concourse.masks as masks
+import concourse.mybir as mybir
+
+F32 = mybir.dt.float32
+BF16 = mybir.dt.bfloat16
+U32 = mybir.dt.uint32
+U8 = mybir.dt.uint8
+FP8X4 = mybir.dt.float8_e4m3fn_x4
+ALU = mybir.AluOpType
+ACT = mybir.ActivationFunctionType
+AX = mybir.AxisListType
+
+P = 128
+B = 4096
+F = 1024
+D = 512
+N = 512
+TILES = B // P
+GROUPS = 8
+FLOPS = 2 * B * F * D + 2 * B * D * N
+
+DIFF = (("v", 0, 2048), ("g", 2048, 2048))
+XCOPY = ("v", "v", "v", "v")
+ECOPY = ("s", "s", "s", "s")
+IN_BUFS = 4
+
+
+def tile_privacyloss_t_kernel(tc, x, y, W, lookup, out):
+    nc = tc.nc
+    xv = x.rearrange("(p c) a h w -> p c (a h w)", c=TILES)
+    yv = y.rearrange("(p c) a h w -> p c (a h w)", c=TILES)
+
+    with ExitStack() as ctx:
+        keep = ctx.enter_context(tc.tile_pool(name="keep", bufs=1))
+        xin = ctx.enter_context(tc.tile_pool(name="xin", bufs=IN_BUFS))
+        work = ctx.enter_context(tc.tile_pool(name="work", bufs=2))
+        dpool = ctx.enter_context(tc.tile_pool(name="dpool", bufs=3))
+        psum = ctx.enter_context(tc.psum_pool(name="psum", bufs=2))
+
+        def copy_on(which, dst, src):
+            if which == "v":
+                nc.vector.tensor_copy(out=dst, in_=src)
+            else:
+                nc.scalar.copy(out=dst, in_=src)
+
+        warm = keep.tile([P, 1], F32)
+        nc.vector.memset(warm[:], 1.0)
+        warm2 = keep.tile([P, 1], F32)
+        nc.scalar.activation(out=warm2[:], in_=warm[:], func=ACT.Sqrt)
+        identf = keep.tile([P, P], F32)
+        masks.make_identity(nc, identf[:])
+        ones = keep.tile([P, P], F32)
+        nc.vector.memset(ones[:], 1.0)
+
+        esum = keep.tile([P, TILES], F32)
+        cmax = keep.tile([P, TILES], F32)
+        dacc = keep.tile([P, GROUPS * len(DIFF)], F32)
+
+        xs_of = {}
+        ys_of = {}
+
+        def load_x(g):
+            xs = xin.tile([P, 4, F], BF16, tag="xs", name="xs")
+            nc.sync.dma_start(out=xs[:], in_=xv[:, 4 * g : 4 * g + 4, :])
+            xs_of[g] = xs
+
+        def load_y(g):
+            ys = xin.tile([P, 4, F], BF16, tag="ys", name="ys")
+            nc.sync.dma_start(out=ys[:], in_=yv[:, 4 * g : 4 * g + 4, :])
+            ys_of[g] = ys
+
+        wraw = keep.tile([P, 2, 4, D], BF16)
+        nc.sync.dma_start(
+            out=wraw[:].rearrange("p g (u e) c -> p (g u) (e c)", u=2),
+            in_=W.rearrange("(a q e) c -> q a (e c)", a=4, e=2),
+        )
+        load_x(0)
+        lk = keep.tile([P, 4, D], BF16)
+        nc.sync.dma_start(out=lk[:], in_=lookup.rearrange("(j b) k -> j b k", b=4))
+        load_y(0)
+        for g in range(1, IN_BUFS):
+            load_x(g)
+            load_y(g)
+
+        wgrp = keep.tile([P, 2, D, 4], BF16, align_bytes=64)
+        for g in range(2):
+            nc.vector.tensor_copy(
+                out=wgrp[:, g].rearrange("p (t m) j -> p t m j", t=4),
+                in_=wraw[:, g].rearrange("p j (m t) -> p t m j", t=4),
+            )
+        wc = keep.tile([P, 2 * D], U32, align_bytes=64)
+        wsc = keep.tile([P, 2 * D], U8, align_bytes=64)
+        nc.vector.quantize_mx(
+            out=wc[:].bitcast(FP8X4),
+            scales=wsc[:],
+            in_=wgrp[:].rearrange("p g w j -> p (g w j)"),
+        )
+
+        lsq = keep.tile([P, 4], F32)
+        for b in range(4):
+            junk = work.tile([P, 2048], BF16, tag="junk", name="junk")
+            nc.scalar.activation(
+                out=junk[:, 0:D], in_=lk[:, b, :], func=ACT.Square, accum_out=lsq[:, b : b + 1]
+            )
+        lhalf = keep.tile([P, 4], F32)
+        nc.vector.tensor_scalar_mul(out=lhalf[:], in0=lsq[:], scalar1=0.5)
+        lkw = lk[:].bitcast(F32).rearrange("p b (w u) -> p b u w", u=2)
+        lgrp = keep.tile([P, N, 4], BF16, align_bytes=64)
+        lg32 = lgrp[:].bitcast(F32)
+        for half in range(2):
+            lt = psum.tile([P, 2, 256], F32, tag="xt", name="lt")
+            for bb in range(2):
+                for u in range(2):
+                    nc.tensor.transpose(
+                        out=lt[:, u, bb * P : (bb + 1) * P],
+                        in_=lkw[:, 2 * half + bb, u, :],
+                        identity=identf[:],
+                    )
+            nc.vector.tensor_copy(
+                out=lg32[:, half * 256 : (half + 1) * 256, :],
+                in_=lt[:].rearrange("p u w -> p w u"),
+            )
+        lc = keep.tile([P, N], U32, align_bytes=64)
+        lsc = keep.tile([P, N], U8, align_bytes=64)
+        nc.vector.quantize_mx(
+            out=lc[:].bitcast(FP8X4), scales=lsc[:], in_=lgrp[:].rearrange("p w j -> p (w j)")
+        )
+
+        xc_of = {}
+        ec_of = {}
+
+        def xpose(g):
+            xs32 = xs_of[g][:].bitcast(F32)
+            xg = work.tile([P, 2, 512, 4], BF16, tag="xg", name="xg", align_bytes=64)
+            xg32 = xg[:].bitcast(F32)
+            xc = work.tile([P, 2, 512], U32, tag="xc", name="xc", align_bytes=64)
+            xsc = work.tile([P, 2, 512], U8, tag="xsc", name="xsc", align_bytes=64)
+            for kp in range(2):
+                for rp in range(2):
+                    xt = psum.tile([P, 2, 256], F32, tag="xt", name="xt")
+                    for rr in range(2):
+                        for u in range(2):
+                            lo = 256 * kp + 128 * u
+                            nc.tensor.transpose(
+                                out=xt[:, u, rr * P : (rr + 1) * P],
+                                in_=xs32[:, 2 * rp + rr, lo : lo + P],
+                                identity=identf[:],
+                            )
+                    copy_on(
+                        XCOPY[2 * kp + rp],
+                        xg32[:, kp, rp * 256 : (rp + 1) * 256, :],
+                        xt[:].rearrange("p u w -> p w u"),
+                    )
+            for kp in range(2):
+                nc.vector.quantize_mx(
+                    out=xc[:, kp, :].bitcast(FP8X4),
+                    scales=xsc[:, kp, :],
+                    in_=xg[:, kp].rearrange("p w j -> p (w j)"),
+                )
+            xc_of[g] = (xc, xsc)
+
+        def emb(g):
+            xc, xsc = xc_of[g]
+            eg = work.tile([P, 512, 4], BF16, tag="eg", name="eg", align_bytes=64)
+            ec = work.tile([P, 512], U32, tag="ec", name="ec", align_bytes=64)
+            esc = work.tile([P, 512], U8, tag="esc", name="esc", align_bytes=64)
+            for r in range(4):
+                rows = slice(r * P, (r + 1) * P)
+                ea = psum.tile([P, D], F32, tag="ea", name="ea")
+                for kp in range(2):
+                    nc.tensor.matmul_mx(
+                        out=ea[:],
+                        lhsT=xc[:, kp, rows].bitcast(FP8X4),
+                        lhsT_scale=xsc[:, kp, rows],
+                        rhs=wc[:, kp * D : (kp + 1) * D].bitcast(FP8X4),
+                        rhs_scale=wsc[:, kp * D : (kp + 1) * D],
+                        start=(kp == 0),
+                        stop=(kp == 1),
+                    )
+                junk = work.tile([P, 2048], BF16, tag="junk", name="junk")
+                nc.scalar.activation(
+                    out=junk[:, 0:D],
+                    in_=ea[:],
+                    func=ACT.Square,
+                    accum_out=esum[:, 4 * g + r : 4 * g + r + 1],
+                )
+                eb = psum.tile([P, 4, P], F32, tag="eb", name="eb")
+                for t in range(4):
+                    for kp in range(2):
+                        cols = slice(kp * D + t * P, kp * D + (t + 1) * P)
+                        nc.tensor.matmul_mx(
+                            out=eb[:, t, :],
+                            lhsT=wc[:, cols].bitcast(FP8X4),
+                            lhsT_scale=wsc[:, cols],
+                            rhs=xc[:, kp, rows].bitcast(FP8X4),
+                            rhs_scale=xsc[:, kp, rows],
+                            start=(kp == 0),
+                            stop=(kp == 1),
+                        )
+                copy_on(ECOPY[r], eg[:, rows, :], eb[:].rearrange("p t q -> p q t"))
+            nc.vector.quantize_mx(
+                out=ec[:].bitcast(FP8X4), scales=esc[:], in_=eg[:].rearrange("p w j -> p (w j)")
+            )
+            ec_of[g] = (ec, esc)
+
+        def mse_part(g):
+            xf = xs_of[g][:].rearrange("p r k -> p (r k)")
+            yf = ys_of[g][:].rearrange("p r k -> p (r k)")
+            for i, (who, lo, width) in enumerate(DIFF):
+                d = dpool.tile([P, 2048], F32, tag="d", name="d")
+                eng = nc.vector if who == "v" else nc.gpsimd
+                eng.tensor_tensor(
+                    out=d[:, 0:width], in0=xf[:, lo : lo + width], in1=yf[:, lo : lo + width], op=ALU.subtract
+                )
+                junk = work.tile([P, 2048], BF16, tag="junk", name="junk")
+                col = g * len(DIFF) + i
+                nc.scalar.activation(
+                    out=junk[:, 0:width], in_=d[:, 0:width], func=ACT.Square, accum_out=dacc[:, col : col + 1]
+                )
+
+        def dist(g):
+            ec, esc = ec_of[g]
+            run = work.tile([P, 512], F32, tag="run", name="run")
+            for b in range(4):
+                cc = psum.tile([P, 512], F32, tag="cc", name="cc")
+                nc.tensor.matmul_mx(
+                    out=cc[:],
+                    lhsT=lc[:, b * P : (b + 1) * P].bitcast(FP8X4),
+                    lhsT_scale=lsc[:, b * P : (b + 1) * P],
+                    rhs=ec[:].bitcast(FP8X4),
+                    rhs_scale=esc[:],
+                    start=True,
+                    stop=True,
+                )
+                if b == 0:
+                    nc.vector.tensor_scalar(
+                        out=run[:], in0=cc[:], scalar1=lhalf[:, 0:1], scalar2=None, op0=ALU.subtract
+                    )
+                else:
+                    nc.vector.scalar_tensor_tensor(
+                        out=run[:],
+                        in0=cc[:],
+                        scalar=lhalf[:, b : b + 1],
+                        in1=run[:],
+                        op0=ALU.subtract,
+                        op1=ALU.max,
+                    )
+            tt = psum.tile([P, 4, P], F32, tag="cc", name="tt")
+            for r in range(4):
+                nc.tensor.transpose(out=tt[:, r, :], in_=run[:, r * P : (r + 1) * P], identity=identf[:])
+            nc.vector.tensor_reduce(out=cmax[:, 4 * g : 4 * g + 4], in_=tt[:], axis=AX.X, op=ALU.max)
+
+        xpose(0)
+        for i in range(GROUPS):
+            if i + 1 < GROUPS:
+                xpose(i + 1)
+            emb(i)
+            mse_part(i)
+            if i + IN_BUFS < GROUPS:
+                load_x(i + IN_BUFS)
+                load_y(i + IN_BUFS)
+            if i >= 1:
+                dist(i - 1)
+        dist(GROUPS - 1)
+
+        dtot = keep.tile([P, 1], F32)
+        nc.vector.tensor_reduce(out=dtot[:], in_=dacc[:], axis=AX.X, op=ALU.add)
+        ms = psum.tile([P, 512], F32, tag="cc", name="ms")
+        nc.tensor.matmul(out=ms[:, 0:1], lhsT=ones[:], rhs=dtot[:], start=True, stop=True)
+        mse = keep.tile([P, 1], F32)
+        nc.vector.tensor_scalar_mul(out=mse[:], in0=ms[:, 0:1], scalar1=1.0 / (B * F))
+
+        sq = keep.tile([P, TILES], F32)
+        nc.vector.scalar_tensor_tensor(
+            out=sq[:], in0=cmax[:], scalar=-2.0, in1=esum[:], op0=ALU.mult, op1=ALU.add
+        )
+        nc.vector.tensor_scalar_max(out=sq[:], in0=sq[:], scalar1=0.0)
+        dmin = keep.tile([P, TILES], F32)
+        nc.scalar.activation(out=dmin[:], in_=sq[:], func=ACT.Sqrt)
+        res = keep.tile([P, TILES], F32)
+        nc.vector.tensor_scalar(
+            out=res[:], in0=dmin[:], scalar1=-1.0, scalar2=50.0, op0=ALU.mult, op1=ALU.add
+        )
+        nc.vector.tensor_scalar(out=res[:], in0=res[:], scalar1=0.0, scalar2=5.0, op0=ALU.min, op1=ALU.mult)
+        nc.vector.tensor_scalar(out=res[:], in0=res[:], scalar1=mse[:, 0:1], scalar2=None, op0=ALU.add)
+        nc.sync.dma_start(out=out.rearrange("(p c) -> p c", c=TILES), in_=res[:])

@@ -21,8 +21,8 @@ TILES = B // P
 GROUPS = 8
 FLOPS = 2 * B * F * D + 2 * B * D * N
 
-DIFF = (("v", 0, 2048), ("g", 2048, 2048))
-XCOPY = ("v", "v", "v", "v")
+DIFF = (("v", 0, 2048), ("v", 2048, 2048))
+XCOPY = ("v", "s", "v", "s")
 ECOPY = ("s", "s", "s", "s")
 IN_BUFS = 4
 

@@ -21,10 +21,45 @@ TILES = B // P
 GROUPS = 8
 FLOPS = 2 * B * F * D + 2 * B * D * N
 
-DIFF = (("v", 0, 2048), ("v", 2048, 2048))
-XCOPY = ("v", "s", "v", "s")
-ECOPY = ("s", "s", "s", "s")
-IN_BUFS = 4
+IN_BUFS = 6
+D_BUFS = 5
+LAG_T = 6
+D_QX = 1
+LAG_QE = 4
+LAG_C = 5
+LAG_ST = 5
+LAG_TT = 12
+LAG_RD = 12
+L_STEP = 0
+SD_LAG = 3
+MSE_LAG = 0
+DF_W = 1024
+DF_PLAN = ((0, 0), (1, 1), (3, 2),)
+DM_PLAN = ((0, 0), (3, 1),)
+XM = 8
+SM = 4
+EM = 0
+PE_ORDER = ("A", "B", "C", "DM", "T", "TT")
+S_ORDER = ("SD", "SA", "EC", "SM", "XS", "S0")
+V_ORDER = ("DF", "ST", "QX", "EV", "QE", "XC", "RD")
+NDM = len(DM_PLAN)
+NACC = NDM + len(DF_PLAN)
+
+
+def xc_on_scalar(g, b):
+    return g == 0 or (XM > 0 and (4 * g + b) % XM == 0)
+
+
+def st0_on_scalar(g):
+    return SM > 0 and g % SM == 0
+
+
+def ec_on_vector(g, r):
+    return EM > 0 and (4 * g + r) % EM == 1
+
+
+def ok(g):
+    return 0 <= g < GROUPS
 
 
 def tile_privacyloss_t_kernel(tc, x, y, W, lookup, out):
@@ -36,14 +71,9 @@ def tile_privacyloss_t_kernel(tc, x, y, W, lookup, out):
         keep = ctx.enter_context(tc.tile_pool(name="keep", bufs=1))
         xin = ctx.enter_context(tc.tile_pool(name="xin", bufs=IN_BUFS))
         work = ctx.enter_context(tc.tile_pool(name="work", bufs=2))
-        dpool = ctx.enter_context(tc.tile_pool(name="dpool", bufs=3))
+        dpool = ctx.enter_context(tc.tile_pool(name="dpool", bufs=D_BUFS))
         psum = ctx.enter_context(tc.psum_pool(name="psum", bufs=2))
-
-        def copy_on(which, dst, src):
-            if which == "v":
-                nc.vector.tensor_copy(out=dst, in_=src)
-            else:
-                nc.scalar.copy(out=dst, in_=src)
+        ctx.enter_context(tc.manual_schedule())
 
         warm = keep.tile([P, 1], F32)
         nc.vector.memset(warm[:], 1.0)
@@ -51,44 +81,48 @@ def tile_privacyloss_t_kernel(tc, x, y, W, lookup, out):
         nc.scalar.activation(out=warm2[:], in_=warm[:], func=ACT.Sqrt)
         identf = keep.tile([P, P], F32)
         masks.make_identity(nc, identf[:])
+        identb = keep.tile([P, P], BF16)
+        masks.make_identity(nc, identb[:])
         ones = keep.tile([P, P], F32)
         nc.vector.memset(ones[:], 1.0)
+        negb = keep.tile([P, P], BF16)
 
         esum = keep.tile([P, TILES], F32)
         cmax = keep.tile([P, TILES], F32)
-        dacc = keep.tile([P, GROUPS * len(DIFF)], F32)
+        dacc = keep.tile([P, GROUPS * NACC], F32)
 
-        xs_of = {}
-        ys_of = {}
+        st = {}
 
         def load_x(g):
             xs = xin.tile([P, 4, F], BF16, tag="xs", name="xs")
             nc.sync.dma_start(out=xs[:], in_=xv[:, 4 * g : 4 * g + 4, :])
-            xs_of[g] = xs
+            st[("xs", g)] = xs
 
         def load_y(g):
             ys = xin.tile([P, 4, F], BF16, tag="ys", name="ys")
             nc.sync.dma_start(out=ys[:], in_=yv[:, 4 * g : 4 * g + 4, :])
-            ys_of[g] = ys
+            st[("ys", g)] = ys
 
         wraw = keep.tile([P, 2, 4, D], BF16)
-        nc.sync.dma_start(
-            out=wraw[:].rearrange("p g (u e) c -> p (g u) (e c)", u=2),
-            in_=W.rearrange("(a q e) c -> q a (e c)", a=4, e=2),
-        )
+        wview = W.rearrange("(a q e) c -> q a (e c)", a=4, e=2)
+        wdst = wraw[:].rearrange("p g (u e) c -> p (g u) (e c)", u=2)
+        for kp in range(2):
+            nc.sync.dma_start(out=wdst[:, 2 * kp : 2 * kp + 2, :], in_=wview[:, 2 * kp : 2 * kp + 2, :])
         load_x(0)
+        load_x(1)
         lk = keep.tile([P, 4, D], BF16)
         nc.sync.dma_start(out=lk[:], in_=lookup.rearrange("(j b) k -> j b k", b=4))
-        load_y(0)
-        for g in range(1, IN_BUFS):
+        for g in range(2, IN_BUFS):
+            load_y(g - 2)
             load_x(g)
-            load_y(g)
+        load_y(IN_BUFS - 2)
+        load_y(IN_BUFS - 1)
 
         wgrp = keep.tile([P, 2, D, 4], BF16, align_bytes=64)
-        for g in range(2):
+        for kp in range(2):
             nc.vector.tensor_copy(
-                out=wgrp[:, g].rearrange("p (t m) j -> p t m j", t=4),
-                in_=wraw[:, g].rearrange("p j (m t) -> p t m j", t=4),
+                out=wgrp[:, kp].rearrange("p (t m) j -> p t m j", t=4),
+                in_=wraw[:, kp].rearrange("p j (m t) -> p t m j", t=4),
             )
         wc = keep.tile([P, 2 * D], U32, align_bytes=64)
         wsc = keep.tile([P, 2 * D], U8, align_bytes=64)
@@ -97,173 +131,323 @@ def tile_privacyloss_t_kernel(tc, x, y, W, lookup, out):
             scales=wsc[:],
             in_=wgrp[:].rearrange("p g w j -> p (g w j)"),
         )
+        nc.vector.tensor_scalar_mul(out=negb[:], in0=identb[:], scalar1=-1.0)
 
         lsq = keep.tile([P, 4], F32)
-        for b in range(4):
-            junk = work.tile([P, 2048], BF16, tag="junk", name="junk")
-            nc.scalar.activation(
-                out=junk[:, 0:D], in_=lk[:, b, :], func=ACT.Square, accum_out=lsq[:, b : b + 1]
-            )
         lhalf = keep.tile([P, 4], F32)
-        nc.vector.tensor_scalar_mul(out=lhalf[:], in0=lsq[:], scalar1=0.5)
-        lkw = lk[:].bitcast(F32).rearrange("p b (w u) -> p b u w", u=2)
         lgrp = keep.tile([P, N, 4], BF16, align_bytes=64)
-        lg32 = lgrp[:].bitcast(F32)
-        for half in range(2):
-            lt = psum.tile([P, 2, 256], F32, tag="xt", name="lt")
-            for bb in range(2):
-                for u in range(2):
-                    nc.tensor.transpose(
-                        out=lt[:, u, bb * P : (bb + 1) * P],
-                        in_=lkw[:, 2 * half + bb, u, :],
-                        identity=identf[:],
-                    )
-            nc.vector.tensor_copy(
-                out=lg32[:, half * 256 : (half + 1) * 256, :],
-                in_=lt[:].rearrange("p u w -> p w u"),
-            )
         lc = keep.tile([P, N], U32, align_bytes=64)
         lsc = keep.tile([P, N], U8, align_bytes=64)
-        nc.vector.quantize_mx(
-            out=lc[:].bitcast(FP8X4), scales=lsc[:], in_=lgrp[:].rearrange("p w j -> p (w j)")
-        )
 
-        xc_of = {}
-        ec_of = {}
+        def new_junk():
+            return work.tile([P, 1024], BF16, tag="junk", name="junk")
 
-        def xpose(g):
-            xs32 = xs_of[g][:].bitcast(F32)
-            xg = work.tile([P, 2, 512, 4], BF16, tag="xg", name="xg", align_bytes=64)
-            xg32 = xg[:].bitcast(F32)
+        def prep_lookup():
+            for b in range(4):
+                junk = new_junk()
+                nc.scalar.activation(
+                    out=junk[:, 0:D], in_=lk[:, b, :], func=ACT.Square, accum_out=lsq[:, b : b + 1]
+                )
+            lkw = lk[:].bitcast(F32).rearrange("p b (w u) -> p b u w", u=2)
+            lg32 = lgrp[:].bitcast(F32)
+            for half in range(2):
+                lt = psum.tile([P, 2, 256], F32, tag="xt", name="lt")
+                for bb in range(2):
+                    for u in range(2):
+                        nc.tensor.transpose(
+                            out=lt[:, u, bb * P : (bb + 1) * P],
+                            in_=lkw[:, 2 * half + bb, u, :],
+                            identity=identf[:],
+                        )
+                nc.vector.tensor_copy(
+                    out=lg32[:, half * 256 : (half + 1) * 256, :],
+                    in_=lt[:].rearrange("p u w -> p w u"),
+                )
+            nc.vector.quantize_mx(
+                out=lc[:].bitcast(FP8X4), scales=lsc[:], in_=lgrp[:].rearrange("p w j -> p (w j)")
+            )
+
+        def op_t(g, b):
+            kp = b // 2
+            rp = b % 2
+            xs32 = st[("xs", g)][:].bitcast(F32)
+            xt = psum.tile([P, 2, 256], F32, tag="xt", name="xt")
+            for rr in range(2):
+                for u in range(2):
+                    lo = 256 * kp + 128 * u
+                    nc.tensor.transpose(
+                        out=xt[:, u, rr * P : (rr + 1) * P],
+                        in_=xs32[:, 2 * rp + rr, lo : lo + P],
+                        identity=identf[:],
+                    )
+            st[("xt", g, b)] = xt
+
+        def op_xc(g, b):
+            kp = b // 2
+            rp = b % 2
+            if ("xg", g) not in st:
+                st[("xg", g)] = work.tile([P, 2, 512, 4], BF16, tag="xg", name="xg", align_bytes=64)
+            xg32 = st[("xg", g)][:].bitcast(F32)
+            dst = xg32[:, kp, rp * 256 : (rp + 1) * 256, :]
+            src = st[("xt", g, b)][:].rearrange("p u w -> p w u")
+            if xc_on_scalar(g, b):
+                nc.scalar.copy(out=dst, in_=src)
+            else:
+                nc.vector.tensor_copy(out=dst, in_=src)
+
+        def op_qx(g):
+            xg = st[("xg", g)]
             xc = work.tile([P, 2, 512], U32, tag="xc", name="xc", align_bytes=64)
             xsc = work.tile([P, 2, 512], U8, tag="xsc", name="xsc", align_bytes=64)
-            for kp in range(2):
-                for rp in range(2):
-                    xt = psum.tile([P, 2, 256], F32, tag="xt", name="xt")
-                    for rr in range(2):
-                        for u in range(2):
-                            lo = 256 * kp + 128 * u
-                            nc.tensor.transpose(
-                                out=xt[:, u, rr * P : (rr + 1) * P],
-                                in_=xs32[:, 2 * rp + rr, lo : lo + P],
-                                identity=identf[:],
-                            )
-                    copy_on(
-                        XCOPY[2 * kp + rp],
-                        xg32[:, kp, rp * 256 : (rp + 1) * 256, :],
-                        xt[:].rearrange("p u w -> p w u"),
-                    )
             for kp in range(2):
                 nc.vector.quantize_mx(
                     out=xc[:, kp, :].bitcast(FP8X4),
                     scales=xsc[:, kp, :],
                     in_=xg[:, kp].rearrange("p w j -> p (w j)"),
                 )
-            xc_of[g] = (xc, xsc)
+            st[("xc", g)] = (xc, xsc)
 
-        def emb(g):
-            xc, xsc = xc_of[g]
-            eg = work.tile([P, 512, 4], BF16, tag="eg", name="eg", align_bytes=64)
-            ec = work.tile([P, 512], U32, tag="ec", name="ec", align_bytes=64)
-            esc = work.tile([P, 512], U8, tag="esc", name="esc", align_bytes=64)
-            for r in range(4):
-                rows = slice(r * P, (r + 1) * P)
-                ea = psum.tile([P, D], F32, tag="ea", name="ea")
+        def op_a(g, r):
+            xc, xsc = st[("xc", g)]
+            rows = slice(r * P, (r + 1) * P)
+            ea = psum.tile([P, D], F32, tag="ea", name="ea")
+            for kp in range(2):
+                nc.tensor.matmul_mx(
+                    out=ea[:],
+                    lhsT=xc[:, kp, rows].bitcast(FP8X4),
+                    lhsT_scale=xsc[:, kp, rows],
+                    rhs=wc[:, kp * D : (kp + 1) * D].bitcast(FP8X4),
+                    rhs_scale=wsc[:, kp * D : (kp + 1) * D],
+                    start=(kp == 0),
+                    stop=(kp == 1),
+                )
+            st[("ea", g, r)] = ea
+
+        def op_sa(g, r):
+            junk = new_junk()
+            nc.scalar.activation(
+                out=junk[:, 0:D],
+                in_=st[("ea", g, r)][:],
+                func=ACT.Square,
+                accum_out=esum[:, 4 * g + r : 4 * g + r + 1],
+            )
+
+        def op_b(g, r):
+            xc, xsc = st[("xc", g)]
+            rows = slice(r * P, (r + 1) * P)
+            eb = psum.tile([P, 4, P], F32, tag="eb", name="eb")
+            for t in range(4):
                 for kp in range(2):
+                    cols = slice(kp * D + t * P, kp * D + (t + 1) * P)
                     nc.tensor.matmul_mx(
-                        out=ea[:],
-                        lhsT=xc[:, kp, rows].bitcast(FP8X4),
-                        lhsT_scale=xsc[:, kp, rows],
-                        rhs=wc[:, kp * D : (kp + 1) * D].bitcast(FP8X4),
-                        rhs_scale=wsc[:, kp * D : (kp + 1) * D],
+                        out=eb[:, t, :],
+                        lhsT=wc[:, cols].bitcast(FP8X4),
+                        lhsT_scale=wsc[:, cols],
+                        rhs=xc[:, kp, rows].bitcast(FP8X4),
+                        rhs_scale=xsc[:, kp, rows],
                         start=(kp == 0),
                         stop=(kp == 1),
                     )
-                junk = work.tile([P, 2048], BF16, tag="junk", name="junk")
-                nc.scalar.activation(
-                    out=junk[:, 0:D],
-                    in_=ea[:],
-                    func=ACT.Square,
-                    accum_out=esum[:, 4 * g + r : 4 * g + r + 1],
-                )
-                eb = psum.tile([P, 4, P], F32, tag="eb", name="eb")
-                for t in range(4):
-                    for kp in range(2):
-                        cols = slice(kp * D + t * P, kp * D + (t + 1) * P)
-                        nc.tensor.matmul_mx(
-                            out=eb[:, t, :],
-                            lhsT=wc[:, cols].bitcast(FP8X4),
-                            lhsT_scale=wsc[:, cols],
-                            rhs=xc[:, kp, rows].bitcast(FP8X4),
-                            rhs_scale=xsc[:, kp, rows],
-                            start=(kp == 0),
-                            stop=(kp == 1),
-                        )
-                copy_on(ECOPY[r], eg[:, rows, :], eb[:].rearrange("p t q -> p q t"))
+            st[("eb", g, r)] = eb
+
+        def op_ec(g, r):
+            if ("eg", g) not in st:
+                st[("eg", g)] = work.tile([P, 512, 4], BF16, tag="eg", name="eg", align_bytes=64)
+            dst = st[("eg", g)][:, r * P : (r + 1) * P, :]
+            src = st[("eb", g, r)][:].rearrange("p t q -> p q t")
+            if ec_on_vector(g, r):
+                nc.vector.tensor_copy(out=dst, in_=src)
+            else:
+                nc.scalar.copy(out=dst, in_=src)
+
+        def op_qe(g):
+            ec = work.tile([P, 512], U32, tag="ec", name="ec", align_bytes=64)
+            esc = work.tile([P, 512], U8, tag="esc", name="esc", align_bytes=64)
             nc.vector.quantize_mx(
-                out=ec[:].bitcast(FP8X4), scales=esc[:], in_=eg[:].rearrange("p w j -> p (w j)")
+                out=ec[:].bitcast(FP8X4),
+                scales=esc[:],
+                in_=st[("eg", g)][:].rearrange("p w j -> p (w j)"),
             )
-            ec_of[g] = (ec, esc)
+            st[("ec", g)] = (ec, esc)
 
-        def mse_part(g):
-            xf = xs_of[g][:].rearrange("p r k -> p (r k)")
-            yf = ys_of[g][:].rearrange("p r k -> p (r k)")
-            for i, (who, lo, width) in enumerate(DIFF):
-                d = dpool.tile([P, 2048], F32, tag="d", name="d")
-                eng = nc.vector if who == "v" else nc.gpsimd
-                eng.tensor_tensor(
-                    out=d[:, 0:width], in0=xf[:, lo : lo + width], in1=yf[:, lo : lo + width], op=ALU.subtract
-                )
-                junk = work.tile([P, 2048], BF16, tag="junk", name="junk")
-                col = g * len(DIFF) + i
-                nc.scalar.activation(
-                    out=junk[:, 0:width], in_=d[:, 0:width], func=ACT.Square, accum_out=dacc[:, col : col + 1]
-                )
+        def op_c(g, b):
+            ec, esc = st[("ec", g)]
+            cc = psum.tile([P, 512], F32, tag="cc", name="cc")
+            nc.tensor.matmul_mx(
+                out=cc[:],
+                lhsT=lc[:, b * P : (b + 1) * P].bitcast(FP8X4),
+                lhsT_scale=lsc[:, b * P : (b + 1) * P],
+                rhs=ec[:].bitcast(FP8X4),
+                rhs_scale=esc[:],
+                start=True,
+                stop=True,
+            )
+            st[("cc", g, b)] = cc
 
-        def dist(g):
-            ec, esc = ec_of[g]
-            run = work.tile([P, 512], F32, tag="run", name="run")
-            for b in range(4):
-                cc = psum.tile([P, 512], F32, tag="cc", name="cc")
-                nc.tensor.matmul_mx(
-                    out=cc[:],
-                    lhsT=lc[:, b * P : (b + 1) * P].bitcast(FP8X4),
-                    lhsT_scale=lsc[:, b * P : (b + 1) * P],
-                    rhs=ec[:].bitcast(FP8X4),
-                    rhs_scale=esc[:],
-                    start=True,
-                    stop=True,
-                )
-                if b == 0:
+        def op_st(g, b):
+            cc = st[("cc", g, b)]
+            if b == 0:
+                run = work.tile([P, 512], F32, tag="run", name="run")
+                st[("run", g)] = run
+                if st0_on_scalar(g):
+                    nc.scalar.activation(out=run[:], in_=cc[:], func=ACT.Identity, bias=lneg[:, 0:1])
+                else:
                     nc.vector.tensor_scalar(
                         out=run[:], in0=cc[:], scalar1=lhalf[:, 0:1], scalar2=None, op0=ALU.subtract
                     )
-                else:
-                    nc.vector.scalar_tensor_tensor(
-                        out=run[:],
-                        in0=cc[:],
-                        scalar=lhalf[:, b : b + 1],
-                        in1=run[:],
-                        op0=ALU.subtract,
-                        op1=ALU.max,
-                    )
+            else:
+                run = st[("run", g)]
+                nc.vector.scalar_tensor_tensor(
+                    out=run[:],
+                    in0=cc[:],
+                    scalar=lhalf[:, b : b + 1],
+                    in1=run[:],
+                    op0=ALU.subtract,
+                    op1=ALU.max,
+                )
+
+        def op_tt(g):
+            run = st[("run", g)]
             tt = psum.tile([P, 4, P], F32, tag="cc", name="tt")
             for r in range(4):
                 nc.tensor.transpose(out=tt[:, r, :], in_=run[:, r * P : (r + 1) * P], identity=identf[:])
-            nc.vector.tensor_reduce(out=cmax[:, 4 * g : 4 * g + 4], in_=tt[:], axis=AX.X, op=ALU.max)
+            st[("tt", g)] = tt
 
-        xpose(0)
-        for i in range(GROUPS):
-            if i + 1 < GROUPS:
-                xpose(i + 1)
-            emb(i)
-            mse_part(i)
-            if i + IN_BUFS < GROUPS:
-                load_x(i + IN_BUFS)
-                load_y(i + IN_BUFS)
-            if i >= 1:
-                dist(i - 1)
-        dist(GROUPS - 1)
+        def op_rd(g):
+            nc.vector.tensor_reduce(
+                out=cmax[:, 4 * g : 4 * g + 4], in_=st[("tt", g)][:], axis=AX.X, op=ALU.max
+            )
+
+        def flat(kind, g):
+            return st[(kind, g)][:].rearrange("p r k -> p (r k)")
+
+        def op_dm(g, k):
+            cols = slice(k * 512, (k + 1) * 512)
+            dm = psum.tile([P, 512], F32, tag="ea", name="dm")
+            nc.tensor.matmul(out=dm[:], lhsT=identb[:], rhs=flat("xs", g)[:, cols], start=True, stop=False)
+            nc.tensor.matmul(out=dm[:], lhsT=negb[:], rhs=flat("ys", g)[:, cols], start=False, stop=True)
+            st[("dm", g, k)] = dm
+
+        def op_sm(g, k):
+            junk = new_junk()
+            col = g * NACC + k
+            nc.scalar.activation(
+                out=junk[:, 0:512], in_=st[("dm", g, k)][:], func=ACT.Square, accum_out=dacc[:, col : col + 1]
+            )
+
+        def op_df(g, k):
+            cols = slice(NDM * 512 + k * DF_W, NDM * 512 + (k + 1) * DF_W)
+            d = dpool.tile([P, DF_W], F32, tag="d", name="d")
+            nc.vector.tensor_tensor(out=d[:], in0=flat("xs", g)[:, cols], in1=flat("ys", g)[:, cols], op=ALU.subtract)
+            st[("d", g, k)] = d
+
+        def op_sd(g, k):
+            junk = new_junk()
+            col = g * NACC + NDM + k
+            nc.scalar.activation(
+                out=junk[:, 0:DF_W], in_=st[("d", g, k)][:], func=ACT.Square, accum_out=dacc[:, col : col + 1]
+            )
+
+        lneg = keep.tile([P, 4], F32)
+        pending = []
+        st["squared"] = 0
+
+        first = -LAG_T - LAG_T % 2
+        last = 4 * GROUPS + max(LAG_RD, LAG_TT, 4 * MSE_LAG + 4) + 2
+        for s in range(first, last):
+            i = s // 4
+            q = s % 4
+            gm = i - MSE_LAG
+            if s == L_STEP:
+                prep_lookup()
+            if s == L_STEP + 3:
+                nc.vector.tensor_scalar_mul(out=lhalf[:], in0=lsq[:], scalar1=0.5)
+                nc.vector.tensor_scalar_mul(out=lneg[:], in0=lsq[:], scalar1=-0.5)
+            banks = [j for j in (s + LAG_T, s + LAG_T + 1) if s % 2 == 0 and j >= 0 and ok(j // 4)]
+            jc = s - LAG_C
+            jst = s - LAG_ST
+            jtt = s - LAG_TT
+            jrd = s - LAG_RD
+            jqe = s - LAG_QE
+            jqx = s + LAG_T - 2 - D_QX
+            for what in PE_ORDER:
+                if what == "T":
+                    for j in banks:
+                        op_t(j // 4, j % 4)
+                elif what == "TT":
+                    if jtt >= 0 and jtt % 4 == 0 and ok(jtt // 4):
+                        op_tt(jtt // 4)
+                elif what == "A":
+                    if ok(i):
+                        op_a(i, q)
+                elif what == "B":
+                    if ok(i):
+                        op_b(i, q)
+                elif what == "C":
+                    if jc >= 0 and ok(jc // 4):
+                        op_c(jc // 4, jc % 4)
+                elif what == "DM":
+                    if ok(gm):
+                        for qq, k in DM_PLAN:
+                            if qq == q:
+                                op_dm(gm, k)
+            for what in S_ORDER:
+                if what == "SA":
+                    if ok(i):
+                        op_sa(i, q)
+                elif what == "EC":
+                    if ok(i) and not ec_on_vector(i, q):
+                        op_ec(i, q)
+                elif what == "SM":
+                    if ok(gm):
+                        for qq, k in DM_PLAN:
+                            if qq == q:
+                                op_sm(gm, k)
+                elif what == "SD":
+                    for rep in range(1 if ok(gm) else 2):
+                        waiting = len(pending) - st["squared"]
+                        if waiting > SD_LAG or (not ok(gm) and waiting > 0):
+                            g0, k0 = pending[st["squared"]]
+                            op_sd(g0, k0)
+                            st["squared"] = st["squared"] + 1
+                elif what == "XS":
+                    for j in banks:
+                        if xc_on_scalar(j // 4, j % 4):
+                            op_xc(j // 4, j % 4)
+                elif what == "S0":
+                    if jst >= 0 and ok(jst // 4) and jst % 4 == 0 and st0_on_scalar(jst // 4):
+                        op_st(jst // 4, 0)
+            for what in V_ORDER:
+                if what == "XC":
+                    for j in banks:
+                        if not xc_on_scalar(j // 4, j % 4):
+                            op_xc(j // 4, j % 4)
+                elif what == "ST":
+                    if jst >= 0 and ok(jst // 4) and not (jst % 4 == 0 and st0_on_scalar(jst // 4)):
+                        op_st(jst // 4, jst % 4)
+                elif what == "EV":
+                    if ok(i) and ec_on_vector(i, q):
+                        op_ec(i, q)
+                elif what == "QE":
+                    if jqe >= 0 and jqe % 4 == 0 and ok(jqe // 4):
+                        op_qe(jqe // 4)
+                elif what == "RD":
+                    if jrd >= 0 and jrd % 4 == 0 and ok(jrd // 4):
+                        op_rd(jrd // 4)
+                elif what == "QX":
+                    if jqx >= 0 and jqx % 4 == 0 and ok(jqx // 4):
+                        op_qx(jqx // 4)
+                elif what == "DF":
+                    if ok(gm):
+                        for qq, k in DF_PLAN:
+                            if qq == q:
+                                op_df(gm, k)
+                                pending.append((gm, k))
+            if q == 3 and ok(gm) and ok(gm + IN_BUFS):
+                load_x(gm + IN_BUFS)
+                load_y(gm + IN_BUFS)
+        for g0, k0 in pending[st["squared"] :]:
+            op_sd(g0, k0)
 
         dtot = keep.tile([P, 1], F32)
         nc.vector.tensor_reduce(out=dtot[:], in_=dacc[:], axis=AX.X, op=ALU.add)
@@ -281,8 +465,9 @@ def tile_privacyloss_t_kernel(tc, x, y, W, lookup, out):
         nc.scalar.activation(out=dmin[:], in_=sq[:], func=ACT.Sqrt)
         res = keep.tile([P, TILES], F32)
         nc.vector.tensor_scalar(
-            out=res[:], in0=dmin[:], scalar1=-1.0, scalar2=50.0, op0=ALU.mult, op1=ALU.add
+            out=res[:], in0=dmin[:], scalar1=-5.0, scalar2=250.0, op0=ALU.mult, op1=ALU.add
         )
-        nc.vector.tensor_scalar(out=res[:], in0=res[:], scalar1=0.0, scalar2=5.0, op0=ALU.min, op1=ALU.mult)
-        nc.vector.tensor_scalar(out=res[:], in0=res[:], scalar1=mse[:, 0:1], scalar2=None, op0=ALU.add)
+        nc.vector.tensor_scalar(
+            out=res[:], in0=res[:], scalar1=0.0, scalar2=mse[:, 0:1], op0=ALU.min, op1=ALU.add
+        )
         nc.sync.dma_start(out=out.rearrange("(p c) -> p c", c=TILES), in_=res[:])

@@ -22,28 +22,36 @@ GROUPS = 8
 FLOPS = 2 * B * F * D + 2 * B * D * N
 
 IN_BUFS = 6
-D_BUFS = 5
+D_BUFS = 6
 LAG_T = 6
 D_QX = 1
-LAG_QE = 4
-LAG_C = 5
-LAG_ST = 5
+LAG_QE = 5
+LAG_C = 7
+LAG_ST = 7
 LAG_TT = 12
-LAG_RD = 12
-L_STEP = 0
-SD_LAG = 3
-MSE_LAG = 0
-DF_W = 1024
-DF_PLAN = ((0, 0), (1, 1), (3, 2),)
-DM_PLAN = ((0, 0), (3, 1),)
-XM = 8
-SM = 4
-EM = 0
+LAG_RD = 13
+L_STEP = -2
+SD_LAG = 0
+MSE_LAG = 1
+DF_W = 768
+DF_PLAN = ((2, 0),)
+G_W = 768
+G_PLAN = ((0, 0), (1, 1), (3, 2),)
+SG_LAG = 0
+SG_PER = 3
+LAG_A = 3
+XC_BUFS = 3
+DM_PLAN = ((0, 0), (2, 1),)
+XM = 4
+SM = 0
+EM = 2
 PE_ORDER = ("A", "B", "C", "DM", "T", "TT")
-S_ORDER = ("SD", "SA", "EC", "SM", "XS", "S0")
-V_ORDER = ("DF", "ST", "QX", "EV", "QE", "XC", "RD")
+S_ORDER = ("SA", "SG", "S0", "SM", "SD", "XS", "EC")
+V_ORDER = ("RD", "DF", "EV", "QE", "ST", "QX", "XC")
 NDM = len(DM_PLAN)
-NACC = NDM + len(DF_PLAN)
+NDF = len(DF_PLAN)
+NACC = NDM + NDF + len(G_PLAN)
+D_W = max(DF_W if NDF > 0 else 0, G_W if len(G_PLAN) > 0 else 0)
 
 
 def xc_on_scalar(g, b):
@@ -109,9 +117,9 @@ def tile_privacyloss_t_kernel(tc, x, y, W, lookup, out):
         for kp in range(2):
             nc.sync.dma_start(out=wdst[:, 2 * kp : 2 * kp + 2, :], in_=wview[:, 2 * kp : 2 * kp + 2, :])
         load_x(0)
-        load_x(1)
         lk = keep.tile([P, 4, D], BF16)
         nc.sync.dma_start(out=lk[:], in_=lookup.rearrange("(j b) k -> j b k", b=4))
+        load_x(1)
         for g in range(2, IN_BUFS):
             load_y(g - 2)
             load_x(g)
@@ -197,8 +205,8 @@ def tile_privacyloss_t_kernel(tc, x, y, W, lookup, out):
 
         def op_qx(g):
             xg = st[("xg", g)]
-            xc = work.tile([P, 2, 512], U32, tag="xc", name="xc", align_bytes=64)
-            xsc = work.tile([P, 2, 512], U8, tag="xsc", name="xsc", align_bytes=64)
+            xc = work.tile([P, 2, 512], U32, tag="xc", name="xc", align_bytes=64, bufs=XC_BUFS)
+            xsc = work.tile([P, 2, 512], U8, tag="xsc", name="xsc", align_bytes=64, bufs=XC_BUFS)
             for kp in range(2):
                 nc.vector.quantize_mx(
                     out=xc[:, kp, :].bitcast(FP8X4),
@@ -337,23 +345,45 @@ def tile_privacyloss_t_kernel(tc, x, y, W, lookup, out):
 
         def op_df(g, k):
             cols = slice(NDM * 512 + k * DF_W, NDM * 512 + (k + 1) * DF_W)
-            d = dpool.tile([P, DF_W], F32, tag="d", name="d")
-            nc.vector.tensor_tensor(out=d[:], in0=flat("xs", g)[:, cols], in1=flat("ys", g)[:, cols], op=ALU.subtract)
+            d = dpool.tile([P, D_W], F32, tag="d", name="d")
+            nc.vector.tensor_tensor(
+                out=d[:, 0:DF_W], in0=flat("xs", g)[:, cols], in1=flat("ys", g)[:, cols], op=ALU.subtract
+            )
             st[("d", g, k)] = d
 
         def op_sd(g, k):
             junk = new_junk()
             col = g * NACC + NDM + k
             nc.scalar.activation(
-                out=junk[:, 0:DF_W], in_=st[("d", g, k)][:], func=ACT.Square, accum_out=dacc[:, col : col + 1]
+                out=junk[:, 0:DF_W], in_=st[("d", g, k)][:, 0:DF_W], func=ACT.Square, accum_out=dacc[:, col : col + 1]
+            )
+
+        def op_dg(g, k):
+            lo = NDM * 512 + NDF * DF_W + k * G_W
+            d = dpool.tile([P, D_W], F32, tag="d", name="d")
+            nc.gpsimd.tensor_tensor(
+                out=d[:, 0:G_W],
+                in0=flat("xs", g)[:, lo : lo + G_W],
+                in1=flat("ys", g)[:, lo : lo + G_W],
+                op=ALU.subtract,
+            )
+            st[("dg", g, k)] = d
+
+        def op_sg(g, k):
+            junk = new_junk()
+            col = g * NACC + NDM + NDF + k
+            nc.scalar.activation(
+                out=junk[:, 0:G_W], in_=st[("dg", g, k)][:, 0:G_W], func=ACT.Square, accum_out=dacc[:, col : col + 1]
             )
 
         lneg = keep.tile([P, 4], F32)
         pending = []
         st["squared"] = 0
+        gpending = []
+        st["gsquared"] = 0
 
         first = -LAG_T - LAG_T % 2
-        last = 4 * GROUPS + max(LAG_RD, LAG_TT, 4 * MSE_LAG + 4) + 2
+        last = 4 * GROUPS + max(LAG_RD, LAG_TT, 4 * MSE_LAG + 4, LAG_A + 1) + 2
         for s in range(first, last):
             i = s // 4
             q = s % 4
@@ -364,6 +394,7 @@ def tile_privacyloss_t_kernel(tc, x, y, W, lookup, out):
                 nc.vector.tensor_scalar_mul(out=lhalf[:], in0=lsq[:], scalar1=0.5)
                 nc.vector.tensor_scalar_mul(out=lneg[:], in0=lsq[:], scalar1=-0.5)
             banks = [j for j in (s + LAG_T, s + LAG_T + 1) if s % 2 == 0 and j >= 0 and ok(j // 4)]
+            ja = s - LAG_A
             jc = s - LAG_C
             jst = s - LAG_ST
             jtt = s - LAG_TT
@@ -378,8 +409,8 @@ def tile_privacyloss_t_kernel(tc, x, y, W, lookup, out):
                     if jtt >= 0 and jtt % 4 == 0 and ok(jtt // 4):
                         op_tt(jtt // 4)
                 elif what == "A":
-                    if ok(i):
-                        op_a(i, q)
+                    if ja >= 0 and ok(ja // 4):
+                        op_a(ja // 4, ja % 4)
                 elif what == "B":
                     if ok(i):
                         op_b(i, q)
@@ -393,8 +424,15 @@ def tile_privacyloss_t_kernel(tc, x, y, W, lookup, out):
                                 op_dm(gm, k)
             for what in S_ORDER:
                 if what == "SA":
-                    if ok(i):
-                        op_sa(i, q)
+                    if ja >= 0 and ok(ja // 4):
+                        op_sa(ja // 4, ja % 4)
+                elif what == "SG":
+                    for rep in range(SG_PER if ok(gm) else 3):
+                        waiting = len(gpending) - st["gsquared"]
+                        if waiting > SG_LAG or (not ok(gm) and waiting > 0):
+                            g0, k0 = gpending[st["gsquared"]]
+                            op_sg(g0, k0)
+                            st["gsquared"] = st["gsquared"] + 1
                 elif what == "EC":
                     if ok(i) and not ec_on_vector(i, q):
                         op_ec(i, q)
@@ -417,6 +455,11 @@ def tile_privacyloss_t_kernel(tc, x, y, W, lookup, out):
                 elif what == "S0":
                     if jst >= 0 and ok(jst // 4) and jst % 4 == 0 and st0_on_scalar(jst // 4):
                         op_st(jst // 4, 0)
+            if ok(gm):
+                for qq, k in G_PLAN:
+                    if qq == q:
+                        op_dg(gm, k)
+                        gpending.append((gm, k))
             for what in V_ORDER:
                 if what == "XC":
                     for j in banks:
@@ -448,6 +491,8 @@ def tile_privacyloss_t_kernel(tc, x, y, W, lookup, out):
                 load_y(gm + IN_BUFS)
         for g0, k0 in pending[st["squared"] :]:
             op_sd(g0, k0)
+        for g0, k0 in gpending[st["gsquared"] :]:
+            op_sg(g0, k0)
 
         dtot = keep.tile([P, 1], F32)
         nc.vector.tensor_reduce(out=dtot[:], in_=dacc[:], axis=AX.X, op=ALU.add)

@@ -25,28 +25,30 @@ IN_BUFS = 6
 D_BUFS = 6
 LAG_T = 6
 D_QX = 1
-LAG_QE = 5
-LAG_C = 7
-LAG_ST = 7
+LAG_QE = 6
+LAG_C = 8
+LAG_ST = 8
 LAG_TT = 12
 LAG_RD = 13
-L_STEP = -2
+L_STEP = 0
 SD_LAG = 0
 MSE_LAG = 1
 DF_W = 768
 DF_PLAN = ((2, 0),)
 G_W = 768
-G_PLAN = ((0, 0), (1, 1), (3, 2),)
+G_PLAN = ((0, 0), (2, 1), (2, 2),)
 SG_LAG = 0
-SG_PER = 3
-LAG_A = 3
+SG_PER = 1
+LAG_A = 2
 XC_BUFS = 3
-DM_PLAN = ((0, 0), (2, 1),)
-XM = 4
+DM_PLAN = ((2, 0), (3, 1),)
+XC_MASK = 1
 SM = 0
-EM = 2
+EC_MASK = 9
+DM_LAG = 2
+BANK_ORDER = (0, 2, 1, 3)
 PE_ORDER = ("A", "B", "C", "DM", "T", "TT")
-S_ORDER = ("SA", "SG", "S0", "SM", "SD", "XS", "EC")
+S_ORDER = ("SA", "SG", "EC", "SM", "XS", "S0", "SD")
 V_ORDER = ("RD", "DF", "EV", "QE", "ST", "QX", "XC")
 NDM = len(DM_PLAN)
 NDF = len(DF_PLAN)
@@ -55,7 +57,7 @@ D_W = max(DF_W if NDF > 0 else 0, G_W if len(G_PLAN) > 0 else 0)
 
 
 def xc_on_scalar(g, b):
-    return g == 0 or (XM > 0 and (4 * g + b) % XM == 0)
+    return g == 0 or (XC_MASK >> b) % 2 == 1
 
 
 def st0_on_scalar(g):
@@ -63,7 +65,7 @@ def st0_on_scalar(g):
 
 
 def ec_on_vector(g, r):
-    return EM > 0 and (4 * g + r) % EM == 1
+    return (EC_MASK >> r) % 2 == 1
 
 
 def ok(g):
@@ -116,10 +118,13 @@ def tile_privacyloss_t_kernel(tc, x, y, W, lookup, out):
         wdst = wraw[:].rearrange("p g (u e) c -> p (g u) (e c)", u=2)
         for kp in range(2):
             nc.sync.dma_start(out=wdst[:, 2 * kp : 2 * kp + 2, :], in_=wview[:, 2 * kp : 2 * kp + 2, :])
-        load_x(0)
+        xs0 = xin.tile([P, 4, F], BF16, tag="xs", name="xs")
+        nc.sync.dma_start(out=xs0[:, 0:2, :], in_=xv[:, 0:2, :])
+        nc.sync.dma_start(out=xs0[:, 2:4, :], in_=xv[:, 2:4, :])
+        st[("xs", 0)] = xs0
+        load_x(1)
         lk = keep.tile([P, 4, D], BF16)
         nc.sync.dma_start(out=lk[:], in_=lookup.rearrange("(j b) k -> j b k", b=4))
-        load_x(1)
         for g in range(2, IN_BUFS):
             load_y(g - 2)
             load_x(g)
@@ -382,12 +387,14 @@ def tile_privacyloss_t_kernel(tc, x, y, W, lookup, out):
         gpending = []
         st["gsquared"] = 0
 
-        first = -LAG_T - LAG_T % 2
-        last = 4 * GROUPS + max(LAG_RD, LAG_TT, 4 * MSE_LAG + 4, LAG_A + 1) + 2
+        first = min(-LAG_T - LAG_T % 2, 4 * min(0, DM_LAG))
+        last = 4 * GROUPS + max(LAG_RD, LAG_TT, 4 * MSE_LAG + 4, 4 * DM_LAG + 4, LAG_A + 1) + 2
         for s in range(first, last):
             i = s // 4
             q = s % 4
             gm = i - MSE_LAG
+            gd = i - DM_LAG
+            gl = i - max(MSE_LAG, DM_LAG)
             if s == L_STEP:
                 prep_lookup()
             if s == L_STEP + 3:
@@ -404,7 +411,7 @@ def tile_privacyloss_t_kernel(tc, x, y, W, lookup, out):
             for what in PE_ORDER:
                 if what == "T":
                     for j in banks:
-                        op_t(j // 4, j % 4)
+                        op_t(j // 4, BANK_ORDER[j % 4])
                 elif what == "TT":
                     if jtt >= 0 and jtt % 4 == 0 and ok(jtt // 4):
                         op_tt(jtt // 4)
@@ -418,10 +425,10 @@ def tile_privacyloss_t_kernel(tc, x, y, W, lookup, out):
                     if jc >= 0 and ok(jc // 4):
                         op_c(jc // 4, jc % 4)
                 elif what == "DM":
-                    if ok(gm):
+                    if ok(gd):
                         for qq, k in DM_PLAN:
                             if qq == q:
-                                op_dm(gm, k)
+                                op_dm(gd, k)
             for what in S_ORDER:
                 if what == "SA":
                     if ja >= 0 and ok(ja // 4):
@@ -437,10 +444,10 @@ def tile_privacyloss_t_kernel(tc, x, y, W, lookup, out):
                     if ok(i) and not ec_on_vector(i, q):
                         op_ec(i, q)
                 elif what == "SM":
-                    if ok(gm):
+                    if ok(gd):
                         for qq, k in DM_PLAN:
                             if qq == q:
-                                op_sm(gm, k)
+                                op_sm(gd, k)
                 elif what == "SD":
                     for rep in range(1 if ok(gm) else 2):
                         waiting = len(pending) - st["squared"]
@@ -450,8 +457,8 @@ def tile_privacyloss_t_kernel(tc, x, y, W, lookup, out):
                             st["squared"] = st["squared"] + 1
                 elif what == "XS":
                     for j in banks:
-                        if xc_on_scalar(j // 4, j % 4):
-                            op_xc(j // 4, j % 4)
+                        if xc_on_scalar(j // 4, BANK_ORDER[j % 4]):
+                            op_xc(j // 4, BANK_ORDER[j % 4])
                 elif what == "S0":
                     if jst >= 0 and ok(jst // 4) and jst % 4 == 0 and st0_on_scalar(jst // 4):
                         op_st(jst // 4, 0)
@@ -463,8 +470,8 @@ def tile_privacyloss_t_kernel(tc, x, y, W, lookup, out):
             for what in V_ORDER:
                 if what == "XC":
                     for j in banks:
-                        if not xc_on_scalar(j // 4, j % 4):
-                            op_xc(j // 4, j % 4)
+                        if not xc_on_scalar(j // 4, BANK_ORDER[j % 4]):
+                            op_xc(j // 4, BANK_ORDER[j % 4])
                 elif what == "ST":
                     if jst >= 0 and ok(jst // 4) and not (jst % 4 == 0 and st0_on_scalar(jst // 4)):
                         op_st(jst // 4, jst % 4)
@@ -486,9 +493,9 @@ def tile_privacyloss_t_kernel(tc, x, y, W, lookup, out):
                             if qq == q:
                                 op_df(gm, k)
                                 pending.append((gm, k))
-            if q == 3 and ok(gm) and ok(gm + IN_BUFS):
-                load_x(gm + IN_BUFS)
-                load_y(gm + IN_BUFS)
+            if q == 3 and ok(gl) and ok(gl + IN_BUFS):
+                load_x(gl + IN_BUFS)
+                load_y(gl + IN_BUFS)
         for g0, k0 in pending[st["squared"] :]:
             op_sd(g0, k0)
         for g0, k0 in gpending[st["gsquared"] :]:

@@ -302,12 +302,9 @@ def tile_privacyloss_t_kernel(tc, x, y, W, lookup, out):
             if b == 0:
                 run = work.tile([P, 512], F32, tag="run", name="run")
                 st[("run", g)] = run
-                if st0_on_scalar(g):
-                    nc.scalar.activation(out=run[:], in_=cc[:], func=ACT.Identity, bias=lneg[:, 0:1])
-                else:
-                    nc.vector.tensor_scalar(
-                        out=run[:], in0=cc[:], scalar1=lhalf[:, 0:1], scalar2=None, op0=ALU.subtract
-                    )
+                nc.vector.tensor_scalar(
+                    out=run[:], in0=cc[:], scalar1=lhalf[:, 0:1], scalar2=None, op0=ALU.subtract
+                )
             else:
                 run = st[("run", g)]
                 nc.vector.scalar_tensor_tensor(
@@ -381,7 +378,6 @@ def tile_privacyloss_t_kernel(tc, x, y, W, lookup, out):
                 out=junk[:, 0:G_W], in_=st[("dg", g, k)][:, 0:G_W], func=ACT.Square, accum_out=dacc[:, col : col + 1]
             )
 
-        lneg = keep.tile([P, 4], F32)
         pending = []
         st["squared"] = 0
         gpending = []
@@ -398,8 +394,7 @@ def tile_privacyloss_t_kernel(tc, x, y, W, lookup, out):
             if s == L_STEP:
                 prep_lookup()
             if s == L_STEP + 3:
-                nc.vector.tensor_scalar_mul(out=lhalf[:], in0=lsq[:], scalar1=0.5)
-                nc.vector.tensor_scalar_mul(out=lneg[:], in0=lsq[:], scalar1=-0.5)
+                nc.scalar.mul(out=lhalf[:], in_=lsq[:], mul=0.5)
             banks = [j for j in (s + LAG_T, s + LAG_T + 1) if s % 2 == 0 and j >= 0 and ok(j // 4)]
             ja = s - LAG_A
             jc = s - LAG_C

@@ -30,7 +30,7 @@ LAG_C = 8
 LAG_ST = 8
 LAG_TT = 12
 LAG_RD = 13
-L_STEP = 0
+L_STEP = 2
 SD_LAG = 0
 MSE_LAG = 1
 DF_W = 768
@@ -57,7 +57,7 @@ D_W = max(DF_W if NDF > 0 else 0, G_W if len(G_PLAN) > 0 else 0)
 
 
 def xc_on_scalar(g, b):
-    return g == 0 or (XC_MASK >> b) % 2 == 1
+    return g < 2 or (XC_MASK >> b) % 2 == 1
 
 
 def st0_on_scalar(g):

@@ -34,8 +34,8 @@ L_STEP = 2
 SD_LAG = 0
 MSE_LAG = 1
 DF_W = 768
-DF_PLAN = ((2, 0),)
-G_W = 768
+DF_PLAN = ()
+G_W = 1024
 G_PLAN = ((0, 0), (2, 1), (2, 2),)
 SG_LAG = 0
 SG_PER = 1
@@ -44,7 +44,7 @@ XC_BUFS = 3
 DM_PLAN = ((2, 0), (3, 1),)
 XC_MASK = 1
 SM = 0
-EC_MASK = 9
+EC_MASK = 11
 DM_LAG = 2
 BANK_ORDER = (0, 2, 1, 3)
 PE_ORDER = ("A", "B", "C", "DM", "T", "TT")

from contextlib import ExitStack

import concourse.masks as masks
import concourse.mybir as mybir

F32 = mybir.dt.float32
BF16 = mybir.dt.bfloat16
U32 = mybir.dt.uint32
U8 = mybir.dt.uint8
FP8X4 = mybir.dt.float8_e4m3fn_x4
ALU = mybir.AluOpType
ACT = mybir.ActivationFunctionType
AX = mybir.AxisListType

P = 128
B = 4096
F = 1024
D = 512
N = 512
TILES = B // P
GROUPS = 8
FLOPS = 2 * B * F * D + 2 * B * D * N

IN_BUFS = 6
D_BUFS = 6
LAG_T = 6
D_QX = 1
LAG_QE = 6
LAG_C = 8
LAG_ST = 8
LAG_TT = 12
LAG_RD = 13
L_STEP = 2
SD_LAG = 0
MSE_LAG = 1
DF_W = 768
DF_PLAN = ()
G_W = 1024
G_PLAN = ((0, 0), (2, 1), (2, 2),)
SG_LAG = 0
SG_PER = 1
LAG_A = 2
XC_BUFS = 3
DM_PLAN = ((2, 0), (3, 1),)
XC_MASK = 1
SM = 0
EC_MASK = 11
DM_LAG = 2
BANK_ORDER = (0, 2, 1, 3)
PE_ORDER = ("A", "B", "C", "DM", "T", "TT")
S_ORDER = ("SA", "SG", "EC", "SM", "XS", "S0", "SD")
V_ORDER = ("RD", "DF", "EV", "QE", "ST", "QX", "XC")
NDM = len(DM_PLAN)
NDF = len(DF_PLAN)
NACC = NDM + NDF + len(G_PLAN)
D_W = max(DF_W if NDF > 0 else 0, G_W if len(G_PLAN) > 0 else 0)


def xc_on_scalar(g, b):
    return g < 2 or (XC_MASK >> b) % 2 == 1


def st0_on_scalar(g):
    return SM > 0 and g % SM == 0


def ec_on_vector(g, r):
    return (EC_MASK >> r) % 2 == 1


def ok(g):
    return 0 <= g < GROUPS


def tile_privacyloss_t_kernel(tc, x, y, W, lookup, out):
    nc = tc.nc
    xv = x.rearrange("(p c) a h w -> p c (a h w)", c=TILES)
    yv = y.rearrange("(p c) a h w -> p c (a h w)", c=TILES)

    with ExitStack() as ctx:
        keep = ctx.enter_context(tc.tile_pool(name="keep", bufs=1))
        xin = ctx.enter_context(tc.tile_pool(name="xin", bufs=IN_BUFS))
        work = ctx.enter_context(tc.tile_pool(name="work", bufs=2))
        dpool = ctx.enter_context(tc.tile_pool(name="dpool", bufs=D_BUFS))
        psum = ctx.enter_context(tc.psum_pool(name="psum", bufs=2))
        ctx.enter_context(tc.manual_schedule())

        warm = keep.tile([P, 1], F32)
        nc.vector.memset(warm[:], 1.0)
        warm2 = keep.tile([P, 1], F32)
        nc.scalar.activation(out=warm2[:], in_=warm[:], func=ACT.Sqrt)
        identf = keep.tile([P, P], F32)
        masks.make_identity(nc, identf[:])
        identb = keep.tile([P, P], BF16)
        masks.make_identity(nc, identb[:])
        ones = keep.tile([P, P], F32)
        nc.vector.memset(ones[:], 1.0)
        negb = keep.tile([P, P], BF16)

        esum = keep.tile([P, TILES], F32)
        cmax = keep.tile([P, TILES], F32)
        dacc = keep.tile([P, GROUPS * NACC], F32)

        st = {}

        def load_x(g):
            xs = xin.tile([P, 4, F], BF16, tag="xs", name="xs")
            nc.sync.dma_start(out=xs[:], in_=xv[:, 4 * g : 4 * g + 4, :])
            st[("xs", g)] = xs

        def load_y(g):
            ys = xin.tile([P, 4, F], BF16, tag="ys", name="ys")
            nc.sync.dma_start(out=ys[:], in_=yv[:, 4 * g : 4 * g + 4, :])
            st[("ys", g)] = ys

        wraw = keep.tile([P, 2, 4, D], BF16)
        wview = W.rearrange("(a q e) c -> q a (e c)", a=4, e=2)
        wdst = wraw[:].rearrange("p g (u e) c -> p (g u) (e c)", u=2)
        for kp in range(2):
            nc.sync.dma_start(out=wdst[:, 2 * kp : 2 * kp + 2, :], in_=wview[:, 2 * kp : 2 * kp + 2, :])
        xs0 = xin.tile([P, 4, F], BF16, tag="xs", name="xs")
        nc.sync.dma_start(out=xs0[:, 0:2, :], in_=xv[:, 0:2, :])
        nc.sync.dma_start(out=xs0[:, 2:4, :], in_=xv[:, 2:4, :])
        st[("xs", 0)] = xs0
        load_x(1)
        lk = keep.tile([P, 4, D], BF16)
        nc.sync.dma_start(out=lk[:], in_=lookup.rearrange("(j b) k -> j b k", b=4))
        for g in range(2, IN_BUFS):
            load_y(g - 2)
            load_x(g)
        load_y(IN_BUFS - 2)
        load_y(IN_BUFS - 1)

        wgrp = keep.tile([P, 2, D, 4], BF16, align_bytes=64)
        for kp in range(2):
            nc.vector.tensor_copy(
                out=wgrp[:, kp].rearrange("p (t m) j -> p t m j", t=4),
                in_=wraw[:, kp].rearrange("p j (m t) -> p t m j", t=4),
            )
        wc = keep.tile([P, 2 * D], U32, align_bytes=64)
        wsc = keep.tile([P, 2 * D], U8, align_bytes=64)
        nc.vector.quantize_mx(
            out=wc[:].bitcast(FP8X4),
            scales=wsc[:],
            in_=wgrp[:].rearrange("p g w j -> p (g w j)"),
        )
        nc.vector.tensor_scalar_mul(out=negb[:], in0=identb[:], scalar1=-1.0)

        lsq = keep.tile([P, 4], F32)
        lhalf = keep.tile([P, 4], F32)
        lgrp = keep.tile([P, N, 4], BF16, align_bytes=64)
        lc = keep.tile([P, N], U32, align_bytes=64)
        lsc = keep.tile([P, N], U8, align_bytes=64)

        def new_junk():
            return work.tile([P, 1024], BF16, tag="junk", name="junk")

        def prep_lookup():
            for b in range(4):
                junk = new_junk()
                nc.scalar.activation(
                    out=junk[:, 0:D], in_=lk[:, b, :], func=ACT.Square, accum_out=lsq[:, b : b + 1]
                )
            lkw = lk[:].bitcast(F32).rearrange("p b (w u) -> p b u w", u=2)
            lg32 = lgrp[:].bitcast(F32)
            for half in range(2):
                lt = psum.tile([P, 2, 256], F32, tag="xt", name="lt")
                for bb in range(2):
                    for u in range(2):
                        nc.tensor.transpose(
                            out=lt[:, u, bb * P : (bb + 1) * P],
                            in_=lkw[:, 2 * half + bb, u, :],
                            identity=identf[:],
                        )
                nc.vector.tensor_copy(
                    out=lg32[:, half * 256 : (half + 1) * 256, :],
                    in_=lt[:].rearrange("p u w -> p w u"),
                )
            nc.vector.quantize_mx(
                out=lc[:].bitcast(FP8X4), scales=lsc[:], in_=lgrp[:].rearrange("p w j -> p (w j)")
            )

        def op_t(g, b):
            kp = b // 2
            rp = b % 2
            xs32 = st[("xs", g)][:].bitcast(F32)
            xt = psum.tile([P, 2, 256], F32, tag="xt", name="xt")
            for rr in range(2):
                for u in range(2):
                    lo = 256 * kp + 128 * u
                    nc.tensor.transpose(
                        out=xt[:, u, rr * P : (rr + 1) * P],
                        in_=xs32[:, 2 * rp + rr, lo : lo + P],
                        identity=identf[:],
                    )
            st[("xt", g, b)] = xt

        def op_xc(g, b):
            kp = b // 2
            rp = b % 2
            if ("xg", g) not in st:
                st[("xg", g)] = work.tile([P, 2, 512, 4], BF16, tag="xg", name="xg", align_bytes=64)
            xg32 = st[("xg", g)][:].bitcast(F32)
            dst = xg32[:, kp, rp * 256 : (rp + 1) * 256, :]
            src = st[("xt", g, b)][:].rearrange("p u w -> p w u")
            if xc_on_scalar(g, b):
                nc.scalar.copy(out=dst, in_=src)
            else:
                nc.vector.tensor_copy(out=dst, in_=src)

        def op_qx(g):
            xg = st[("xg", g)]
            xc = work.tile([P, 2, 512], U32, tag="xc", name="xc", align_bytes=64, bufs=XC_BUFS)
            xsc = work.tile([P, 2, 512], U8, tag="xsc", name="xsc", align_bytes=64, bufs=XC_BUFS)
            for kp in range(2):
                nc.vector.quantize_mx(
                    out=xc[:, kp, :].bitcast(FP8X4),
                    scales=xsc[:, kp, :],
                    in_=xg[:, kp].rearrange("p w j -> p (w j)"),
                )
            st[("xc", g)] = (xc, xsc)

        def op_a(g, r):
            xc, xsc = st[("xc", g)]
            rows = slice(r * P, (r + 1) * P)
            ea = psum.tile([P, D], F32, tag="ea", name="ea")
            for kp in range(2):
                nc.tensor.matmul_mx(
                    out=ea[:],
                    lhsT=xc[:, kp, rows].bitcast(FP8X4),
                    lhsT_scale=xsc[:, kp, rows],
                    rhs=wc[:, kp * D : (kp + 1) * D].bitcast(FP8X4),
                    rhs_scale=wsc[:, kp * D : (kp + 1) * D],
                    start=(kp == 0),
                    stop=(kp == 1),
                )
            st[("ea", g, r)] = ea

        def op_sa(g, r):
            junk = new_junk()
            nc.scalar.activation(
                out=junk[:, 0:D],
                in_=st[("ea", g, r)][:],
                func=ACT.Square,
                accum_out=esum[:, 4 * g + r : 4 * g + r + 1],
            )

        def op_b(g, r):
            xc, xsc = st[("xc", g)]
            rows = slice(r * P, (r + 1) * P)
            eb = psum.tile([P, 4, P], F32, tag="eb", name="eb")
            for t in range(4):
                for kp in range(2):
                    cols = slice(kp * D + t * P, kp * D + (t + 1) * P)
                    nc.tensor.matmul_mx(
                        out=eb[:, t, :],
                        lhsT=wc[:, cols].bitcast(FP8X4),
                        lhsT_scale=wsc[:, cols],
                        rhs=xc[:, kp, rows].bitcast(FP8X4),
                        rhs_scale=xsc[:, kp, rows],
                        start=(kp == 0),
                        stop=(kp == 1),
                    )
            st[("eb", g, r)] = eb

        def op_ec(g, r):
            if ("eg", g) not in st:
                st[("eg", g)] = work.tile([P, 512, 4], BF16, tag="eg", name="eg", align_bytes=64)
            dst = st[("eg", g)][:, r * P : (r + 1) * P, :]
            src = st[("eb", g, r)][:].rearrange("p t q -> p q t")
            if ec_on_vector(g, r):
                nc.vector.tensor_copy(out=dst, in_=src)
            else:
                nc.scalar.copy(out=dst, in_=src)

        def op_qe(g):
            ec = work.tile([P, 512], U32, tag="ec", name="ec", align_bytes=64)
            esc = work.tile([P, 512], U8, tag="esc", name="esc", align_bytes=64)
            nc.vector.quantize_mx(
                out=ec[:].bitcast(FP8X4),
                scales=esc[:],
                in_=st[("eg", g)][:].rearrange("p w j -> p (w j)"),
            )
            st[("ec", g)] = (ec, esc)

        def op_c(g, b):
            ec, esc = st[("ec", g)]
            cc = psum.tile([P, 512], F32, tag="cc", name="cc")
            nc.tensor.matmul_mx(
                out=cc[:],
                lhsT=lc[:, b * P : (b + 1) * P].bitcast(FP8X4),
                lhsT_scale=lsc[:, b * P : (b + 1) * P],
                rhs=ec[:].bitcast(FP8X4),
                rhs_scale=esc[:],
                start=True,
                stop=True,
            )
            st[("cc", g, b)] = cc

        def op_st(g, b):
            cc = st[("cc", g, b)]
            if b == 0:
                run = work.tile([P, 512], F32, tag="run", name="run")
                st[("run", g)] = run
                nc.vector.tensor_scalar(
                    out=run[:], in0=cc[:], scalar1=lhalf[:, 0:1], scalar2=None, op0=ALU.subtract
                )
            else:
                run = st[("run", g)]
                nc.vector.scalar_tensor_tensor(
                    out=run[:],
                    in0=cc[:],
                    scalar=lhalf[:, b : b + 1],
                    in1=run[:],
                    op0=ALU.subtract,
                    op1=ALU.max,
                )

        def op_tt(g):
            run = st[("run", g)]
            tt = psum.tile([P, 4, P], F32, tag="cc", name="tt")
            for r in range(4):
                nc.tensor.transpose(out=tt[:, r, :], in_=run[:, r * P : (r + 1) * P], identity=identf[:])
            st[("tt", g)] = tt

        def op_rd(g):
            nc.vector.tensor_reduce(
                out=cmax[:, 4 * g : 4 * g + 4], in_=st[("tt", g)][:], axis=AX.X, op=ALU.max
            )

        def flat(kind, g):
            return st[(kind, g)][:].rearrange("p r k -> p (r k)")

        def op_dm(g, k):
            cols = slice(k * 512, (k + 1) * 512)
            dm = psum.tile([P, 512], F32, tag="ea", name="dm")
            nc.tensor.matmul(out=dm[:], lhsT=identb[:], rhs=flat("xs", g)[:, cols], start=True, stop=False)
            nc.tensor.matmul(out=dm[:], lhsT=negb[:], rhs=flat("ys", g)[:, cols], start=False, stop=True)
            st[("dm", g, k)] = dm

        def op_sm(g, k):
            junk = new_junk()
            col = g * NACC + k
            nc.scalar.activation(
                out=junk[:, 0:512], in_=st[("dm", g, k)][:], func=ACT.Square, accum_out=dacc[:, col : col + 1]
            )

        def op_df(g, k):
            cols = slice(NDM * 512 + k * DF_W, NDM * 512 + (k + 1) * DF_W)
            d = dpool.tile([P, D_W], F32, tag="d", name="d")
            nc.vector.tensor_tensor(
                out=d[:, 0:DF_W], in0=flat("xs", g)[:, cols], in1=flat("ys", g)[:, cols], op=ALU.subtract
            )
            st[("d", g, k)] = d

        def op_sd(g, k):
            junk = new_junk()
            col = g * NACC + NDM + k
            nc.scalar.activation(
                out=junk[:, 0:DF_W], in_=st[("d", g, k)][:, 0:DF_W], func=ACT.Square, accum_out=dacc[:, col : col + 1]
            )

        def op_dg(g, k):
            lo = NDM * 512 + NDF * DF_W + k * G_W
            d = dpool.tile([P, D_W], F32, tag="d", name="d")
            nc.gpsimd.tensor_tensor(
                out=d[:, 0:G_W],
                in0=flat("xs", g)[:, lo : lo + G_W],
                in1=flat("ys", g)[:, lo : lo + G_W],
                op=ALU.subtract,
            )
            st[("dg", g, k)] = d

        def op_sg(g, k):
            junk = new_junk()
            col = g * NACC + NDM + NDF + k
            nc.scalar.activation(
                out=junk[:, 0:G_W], in_=st[("dg", g, k)][:, 0:G_W], func=ACT.Square, accum_out=dacc[:, col : col + 1]
            )

        pending = []
        st["squared"] = 0
        gpending = []
        st["gsquared"] = 0

        first = min(-LAG_T - LAG_T % 2, 4 * min(0, DM_LAG))
        last = 4 * GROUPS + max(LAG_RD, LAG_TT, 4 * MSE_LAG + 4, 4 * DM_LAG + 4, LAG_A + 1) + 2
        for s in range(first, last):
            i = s // 4
            q = s % 4
            gm = i - MSE_LAG
            gd = i - DM_LAG
            gl = i - max(MSE_LAG, DM_LAG)
            if s == L_STEP:
                prep_lookup()
            if s == L_STEP + 3:
                nc.scalar.mul(out=lhalf[:], in_=lsq[:], mul=0.5)
            banks = [j for j in (s + LAG_T, s + LAG_T + 1) if s % 2 == 0 and j >= 0 and ok(j // 4)]
            ja = s - LAG_A
            jc = s - LAG_C
            jst = s - LAG_ST
            jtt = s - LAG_TT
            jrd = s - LAG_RD
            jqe = s - LAG_QE
            jqx = s + LAG_T - 2 - D_QX
            for what in PE_ORDER:
                if what == "T":
                    for j in banks:
                        op_t(j // 4, BANK_ORDER[j % 4])
                elif what == "TT":
                    if jtt >= 0 and jtt % 4 == 0 and ok(jtt // 4):
                        op_tt(jtt // 4)
                elif what == "A":
                    if ja >= 0 and ok(ja // 4):
                        op_a(ja // 4, ja % 4)
                elif what == "B":
                    if ok(i):
                        op_b(i, q)
                elif what == "C":
                    if jc >= 0 and ok(jc // 4):
                        op_c(jc // 4, jc % 4)
                elif what == "DM":
                    if ok(gd):
                        for qq, k in DM_PLAN:
                            if qq == q:
                                op_dm(gd, k)
            for what in S_ORDER:
                if what == "SA":
                    if ja >= 0 and ok(ja // 4):
                        op_sa(ja // 4, ja % 4)
                elif what == "SG":
                    for rep in range(SG_PER if ok(gm) else 3):
                        waiting = len(gpending) - st["gsquared"]
                        if waiting > SG_LAG or (not ok(gm) and waiting > 0):
                            g0, k0 = gpending[st["gsquared"]]
                            op_sg(g0, k0)
                            st["gsquared"] = st["gsquared"] + 1
                elif what == "EC":
                    if ok(i) and not ec_on_vector(i, q):
                        op_ec(i, q)
                elif what == "SM":
                    if ok(gd):
                        for qq, k in DM_PLAN:
                            if qq == q:
                                op_sm(gd, k)
                elif what == "SD":
                    for rep in range(1 if ok(gm) else 2):
                        waiting = len(pending) - st["squared"]
                        if waiting > SD_LAG or (not ok(gm) and waiting > 0):
                            g0, k0 = pending[st["squared"]]
                            op_sd(g0, k0)
                            st["squared"] = st["squared"] + 1
                elif what == "XS":
                    for j in banks:
                        if xc_on_scalar(j // 4, BANK_ORDER[j % 4]):
                            op_xc(j // 4, BANK_ORDER[j % 4])
                elif what == "S0":
                    if jst >= 0 and ok(jst // 4) and jst % 4 == 0 and st0_on_scalar(jst // 4):
                        op_st(jst // 4, 0)
            if ok(gm):
                for qq, k in G_PLAN:
                    if qq == q:
                        op_dg(gm, k)
                        gpending.append((gm, k))
            for what in V_ORDER:
                if what == "XC":
                    for j in banks:
                        if not xc_on_scalar(j // 4, BANK_ORDER[j % 4]):
                            op_xc(j // 4, BANK_ORDER[j % 4])
                elif what == "ST":
                    if jst >= 0 and ok(jst // 4) and not (jst % 4 == 0 and st0_on_scalar(jst // 4)):
                        op_st(jst // 4, jst % 4)
                elif what == "EV":
                    if ok(i) and ec_on_vector(i, q):
                        op_ec(i, q)
                elif what == "QE":
                    if jqe >= 0 and jqe % 4 == 0 and ok(jqe // 4):
                        op_qe(jqe // 4)
                elif what == "RD":
                    if jrd >= 0 and jrd % 4 == 0 and ok(jrd // 4):
                        op_rd(jrd // 4)
                elif what == "QX":
                    if jqx >= 0 and jqx % 4 == 0 and ok(jqx // 4):
                        op_qx(jqx // 4)
                elif what == "DF":
                    if ok(gm):
                        for qq, k in DF_PLAN:
                            if qq == q:
                                op_df(gm, k)
                                pending.append((gm, k))
            if q == 3 and ok(gl) and ok(gl + IN_BUFS):
                load_x(gl + IN_BUFS)
                load_y(gl + IN_BUFS)
        for g0, k0 in pending[st["squared"] :]:
            op_sd(g0, k0)
        for g0, k0 in gpending[st["gsquared"] :]:
            op_sg(g0, k0)

        dtot = keep.tile([P, 1], F32)
        nc.vector.tensor_reduce(out=dtot[:], in_=dacc[:], axis=AX.X, op=ALU.add)
        ms = psum.tile([P, 512], F32, tag="cc", name="ms")
        nc.tensor.matmul(out=ms[:, 0:1], lhsT=ones[:], rhs=dtot[:], start=True, stop=True)
        mse = keep.tile([P, 1], F32)
        nc.vector.tensor_scalar_mul(out=mse[:], in0=ms[:, 0:1], scalar1=1.0 / (B * F))

        sq = keep.tile([P, TILES], F32)
        nc.vector.scalar_tensor_tensor(
            out=sq[:], in0=cmax[:], scalar=-2.0, in1=esum[:], op0=ALU.mult, op1=ALU.add
        )
        nc.vector.tensor_scalar_max(out=sq[:], in0=sq[:], scalar1=0.0)
        dmin = keep.tile([P, TILES], F32)
        nc.scalar.activation(out=dmin[:], in_=sq[:], func=ACT.Sqrt)
        res = keep.tile([P, TILES], F32)
        nc.vector.tensor_scalar(
            out=res[:], in0=dmin[:], scalar1=-5.0, scalar2=250.0, op0=ALU.mult, op1=ALU.add
        )
        nc.vector.tensor_scalar(
            out=res[:], in0=res[:], scalar1=0.0, scalar2=mse[:, 0:1], op0=ALU.min, op1=ALU.add
        )
        nc.sync.dma_start(out=out.rearrange("(p c) -> p c", c=TILES), in_=res[:])
